import numpy as np
import ml_dtypes


def mxq(x, axis, fmt="e4m3"):
    dtype, down = {"e4m3": (ml_dtypes.float8_e4m3fn, 7), "e5m2": (ml_dtypes.float8_e5m2, 14)}[fmt]
    v = np.moveaxis(np.asarray(x, np.float32).astype(ml_dtypes.bfloat16).astype(np.float64), axis, -1)
    blocks = v.reshape(v.shape[:-1] + (-1, 32))
    amax = np.abs(blocks).max(-1, keepdims=True)
    byte = np.maximum(np.where(amax > 0, np.frexp(amax)[1] - 1 + 127, 0) - down, 1)
    scale = np.exp2(byte - 127.0)
    codes = (blocks / scale).astype(np.float32).astype(dtype).astype(np.float64)
    return np.moveaxis((codes * scale).reshape(v.shape), -1, axis)


WIDE = False


def mx_kscale(k):
    if not WIDE:
        return np.ones(k)
    levels = np.array([10, -10, 5, -5, 0])
    a = np.random.permutation(np.resize(levels, k // 512 * 4)).reshape(k // 512, 4)
    idx = np.arange(k)
    return np.exp2(a[idx // 512, idx % 128 // 32])


BF16 = ml_dtypes.bfloat16


def bf(x):
    return np.asarray(x, np.float32).astype(BF16)


def f64(x):
    return np.asarray(x).astype(np.float64)


B, C, T, V, OUT, REL, TS = 1, 512, 32, 32, 1024, 64, 16
TP = T + TS - 1
K = V * TS


def setup_inputs():
    s = mx_kscale(K)[::TS]
    t = mx_kscale(C)
    return {'x_pad': bf(np.random.standard_normal((B, C, TP, V)) * t[None, :, None, None] * s),
            'rel': bf(np.random.standard_normal((B, C * TS, V, V)) / np.sqrt(K) / s[:, None]),
            'A': bf(np.random.standard_normal((V, V)) * 0.7 / np.sqrt(K) / s[:, None]),
            'w3': bf(np.random.standard_normal((OUT, C)) / np.sqrt(C) / t),
            'b3': bf(np.random.standard_normal(OUT) * 0.3)}


def reference(x_pad, rel, A, w3, b3):
    adj = f64(rel) + f64(A)[None, None]
    W = adj.reshape(B, C, TS, V, V).transpose(0, 1, 3, 2, 4).reshape(B, C, K, V)
    xf = f64(x_pad)
    xw = np.stack([xf[:, :, k:k + T, :] for k in range(TS)], axis=-1).reshape(B, C, T, K)
    z = mxq(xw, 3, 'e4m3') @ mxq(W, 2, 'e4m3')
    y = mxq(f64(w3), 1, 'e4m3') @ mxq(z.reshape(B, C, T * V), 1, 'e4m3')
    return (y + f64(b3)[None, :, None]).reshape(B, OUT, T, V)

@@ -1,0 +1,284 @@
+from contextlib import ExitStack
+
+import concourse.mybir as mybir
+from concourse.masks import make_identity
+
+FLOPS = 2 * 512 * 32 * 512 * 32 + 2 * 1024 * 512 * 1024
+
+BF16 = mybir.dt.bfloat16
+F32 = mybir.dt.float32
+U32 = mybir.dt.uint32
+U8 = mybir.dt.uint8
+FP8X4 = mybir.dt.float8_e4m3fn_x4
+ADD = mybir.AluOpType.add
+IDENTITY = mybir.ActivationFunctionType.Identity
+
+P = 128
+NG = 16
+XG = 4
+FR = 35
+XE = FR * 32
+TPB = 8
+NB = 32 // TPB
+
+
+def tile_gccgc_pa_kernel(tc, x_pad, rel, A, w3, b3, out):
+    nc = tc.nc
+    relv = rel.rearrange("b (n r q) j i -> r (b n) (q j i)", r=P, q=4)
+    xv = x_pad.rearrange("b (n c) f j -> c (b n) (f j)", c=32)
+    w3v = w3.rearrange("(t p) c -> p t c", p=P)
+    b3v = b3.rearrange("(t p) -> t p", p=P)
+    outv = out.rearrange("b (t p) f i -> p (b t) (f i)", p=P)
+
+    with ExitStack() as ctx:
+        ctx.enter_context(tc.manual_schedule())
+        const = ctx.enter_context(tc.tile_pool(name="const", bufs=1))
+        rpool = ctx.enter_context(tc.tile_pool(name="rpool", bufs=3))
+        work = ctx.enter_context(tc.tile_pool(name="work", bufs=2))
+        ypool = ctx.enter_context(tc.tile_pool(name="ypool", bufs=4))
+        psw = ctx.enter_context(tc.psum_pool(name="psw", bufs=3))
+        psx = ctx.enter_context(tc.psum_pool(name="psx", bufs=3))
+        psz = ctx.enter_context(tc.psum_pool(name="psz", bufs=2))
+
+        r_t, pn_t, xt_t, xp_t = {}, {}, {}, {}
+        inw_t, inx_t, q_t = {}, {}, {}
+
+        def load_rel(n):
+            r = rpool.tile([P, 4096], BF16, name="r")
+            nc.sync.dma_start(out=r[:], in_=relv[:, n, :])
+            r_t[n] = r
+
+        def load_x(k):
+            xt = work.tile([P, XG * XE], BF16, name="xt")
+            xtv = xt[:].rearrange("p (n e) -> p n e", n=XG)
+            for tt in range(4):
+                nc.sync.dma_start(
+                    out=xtv[tt:P:4, :, :], in_=xv[:, XG * k : XG * (k + 1), 128 * tt : 128 * tt + XE]
+                )
+            xt_t[k] = xt
+            xp_t[k] = work.tile([P, XG * XE], BF16, name="xp")
+
+        def perm_x(n, eng):
+            k, e0 = n // XG, (n % XG) * XE
+            dst = xp_t[k][:, e0 : e0 + XE].rearrange("p (f m a) -> p f m a", m=8, a=4)
+            src = xt_t[k][:, e0 : e0 + XE].rearrange("p (f a m) -> p f m a", m=8, a=4)
+            if eng == "v":
+                nc.vector.tensor_copy(out=dst, in_=src)
+            else:
+                nc.scalar.copy(out=dst, in_=src)
+
+        def perm_w(n, kq):
+            if kq == 0:
+                pn_t[n] = work.tile([P, 4096], BF16, name="pn")
+            nc.vector.tensor_copy(
+                out=pn_t[n][:].bitcast(F32).rearrange("p (w q m a) -> p q m w a", w=16, q=4, m=8, a=4)[:, kq],
+                in_=r_t[n][:].bitcast(F32).rearrange("p (q a m w) -> p q m w a", q=4, a=4, m=8, w=16)[:, kq],
+            )
+
+        az = const.tile([P, P], BF16, name="az")
+        nc.vector.memset(az[:], 0.0)
+        bz = const.tile([P, P], BF16, name="bz")
+        nc.vector.memset(bz[:], 0.0)
+        nc.sync.dma_start(out=az[0:32, 0:32], in_=A)
+        load_x(0)
+        load_rel(0)
+        load_rel(1)
+        load_x(1)
+        nc.sync.dma_start(out=bz[0:8, :], in_=b3v)
+
+        ident_b = const.tile([P, P], BF16, name="ident_b")
+        make_identity(nc, ident_b[:])
+        ident_f = const.tile([P, P], F32, name="ident_f")
+        make_identity(nc, ident_f[:])
+
+        ps1 = psz.tile([P, P], BF16, name="ps1", tag="zp")
+        nc.tensor.transpose(ps1[:], az[:], ident_b[:])
+        atr = const.tile([P, P], BF16, name="atr")
+        nc.vector.tensor_copy(
+            out=atr[:].rearrange("p (q m a) -> p q m a", q=4, m=8, a=4),
+            in_=ps1[:, 0:32].rearrange("p (a m) -> p m a", a=4).unsqueeze(1).to_broadcast([P, 4, 8, 4]),
+        )
+        ps2 = psz.tile([P, P], BF16, name="ps2", tag="zp")
+        nc.tensor.transpose(ps2[:], atr[:], ident_b[:])
+        arep = const.tile([P, P], BF16, name="arep")
+        nc.vector.tensor_copy(
+            out=arep[:].rearrange("p (i t) -> p i t", t=4),
+            in_=ps2[:, 0:32].unsqueeze(2).to_broadcast([P, 32, 4]),
+        )
+        acol = const.tile([P, 32], F32, name="acol")
+        nc.vector.tensor_copy(out=acol[:], in_=ps2[:, 0:32])
+
+        for n in range(XG):
+            perm_x(n, "v")
+            perm_w(0, n)
+
+        zc = const.tile([P, 4096], F32, name="zc")
+        zcv = zc[:].rearrange("p (i g) -> p i g", g=P)
+        b3f = const.tile([P, 8], F32, name="b3f")
+        w3c = const.tile([P, 1024], U32, name="w3c", align_bytes=64)
+        w3s = const.tile([P, 1024], U8, name="w3s", align_bytes=64)
+        w3r = const.tile([P, 4096], BF16, name="w3r")
+        w3w = w3r[:].bitcast(F32).rearrange("p (t q u) -> p t q u", t=8, q=P, u=2)
+        inw3 = const.tile([P, 4096], BF16, name="inw3", align_bytes=64)
+        inw3w = inw3[:].bitcast(F32).rearrange("p (t o u) -> p t o u", t=8, o=P, u=2)
+
+        def prepare_b3():
+            ps3 = psz.tile([P, P], BF16, name="ps3", tag="zp")
+            nc.tensor.transpose(ps3[:], bz[:], ident_b[:])
+            nc.scalar.copy(out=b3f[:], in_=ps3[:, 0:8])
+
+        def prepare_w3(tp):
+            w3p = psz.tile([P, 512], F32, name="w3p", tag="zp")
+            for s in range(4):
+                nc.tensor.transpose(w3p[:, s * P : (s + 1) * P], w3w[:, 2 * tp + s // 2, :, s % 2], ident_f[:])
+            nc.scalar.copy(
+                out=inw3w[:, 2 * tp : 2 * tp + 2, :, :],
+                in_=w3p[:].rearrange("p (t u o) -> p t o u", t=2, u=2, o=P),
+            )
+
+        def first_products(n, engines):
+            xc, xs, wc, ws = q_t[n]
+            for hb in range(2):
+                zp = psz.tile([P, 512], F32, name="zp")
+                for s in range(4):
+                    cols = slice((4 * hb + s) * P, (4 * hb + s + 1) * P)
+                    nc.tensor.matmul_mx(
+                        out=zp[:, s * P : (s + 1) * P],
+                        lhsT=xc[:, cols].bitcast(FP8X4),
+                        lhsT_scale=xs[:, cols],
+                        rhs=wc[:, cols].bitcast(FP8X4),
+                        rhs_scale=ws[:, cols],
+                        start=True,
+                        stop=True,
+                    )
+                g0 = 8 * n + 4 * hb
+                for c4 in range(4):
+                    rows = slice(32 * c4, 32 * c4 + 32)
+                    dst = zcv[rows, :, g0 : g0 + 4]
+                    src = zp[rows, :].rearrange("p (g c i) -> p c i g", g=4, c=4, i=32)[:, c4, :, :]
+                    if engines[c4] == "v":
+                        nc.vector.tensor_copy(out=dst, in_=src)
+                    else:
+                        nc.scalar.copy(out=dst, in_=src)
+
+        def quantise(n, piece):
+            if piece == 0:
+                q_t[n] = (
+                    work.tile([P, 1024], U32, name="xc", align_bytes=64),
+                    work.tile([P, 1024], U8, name="xs", align_bytes=64),
+                    work.tile([P, 1024], U32, name="wc", align_bytes=64),
+                    work.tile([P, 1024], U8, name="ws", align_bytes=64),
+                )
+            xc, xs, wc, ws = q_t[n]
+            h = piece // 2
+            codes, scales, values = (xc, xs, inx_t[n]) if piece % 2 == 0 else (wc, ws, inw_t[n])
+            nc.vector.quantize_mx(
+                out=codes[:, 512 * h : 512 * (h + 1)].bitcast(FP8X4),
+                scales=scales[:, 512 * h : 512 * (h + 1)],
+                in_=values[:, 2048 * h : 2048 * (h + 1)],
+            )
+
+        for n in range(NG + 1):
+            if n + 2 < NG:
+                load_rel(n + 2)
+            if n % XG == XG - 1 and n // XG + 2 < NG // XG:
+                load_x(n // XG + 2)
+            if n == 1:
+                nc.sync.dma_start(out=w3r[:].rearrange("p (t c) -> p t c", t=8), in_=w3v)
+            if n < NG:
+                pv = pn_t[n][:].rearrange("p (w q h) -> p w q h", w=16, q=P, h=2)
+                xp = xp_t[n // XG]
+                x0 = (n % XG) * XE
+                inw_t[n] = work.tile([P, 4096], BF16, name="inw", align_bytes=64)
+                inwv = inw_t[n][:].rearrange("p (c i t) -> p c i t", c=32, i=32, t=4)
+                inx_t[n] = work.tile([P, 4096], BF16, name="inx", align_bytes=64)
+                inxw = inx_t[n][:].bitcast(F32).rearrange("p (c t u) -> p c t u", c=32, t=32, u=2)
+            for b in range(NB):
+                if n < NG:
+                    wtp = psw.tile([P, TPB * P], BF16, name="wtp")
+                    for s in range(TPB):
+                        i = TPB * b + s
+                        nc.tensor.transpose(wtp[:, s * P : (s + 1) * P], pv[:, i // 2, :, i % 2], ident_b[:])
+                    xtp = psx.tile([P, TPB * P], BF16, name="xtp")
+                    for s in range(TPB):
+                        t = TPB * b + s
+                        nc.tensor.transpose(
+                            xtp[:, s * P : (s + 1) * P], xp[:, x0 + 32 * t : x0 + 32 * t + P], ident_b[:]
+                        )
+                    nc.vector.tensor_tensor(
+                        out=inwv[:, :, TPB * b : TPB * (b + 1), :],
+                        in0=wtp[:].rearrange("p (s c t) -> p c s t", s=TPB, c=32, t=4),
+                        in1=arep[:, 4 * TPB * b : 4 * TPB * (b + 1)]
+                        .rearrange("p (s t) -> p s t", t=4)
+                        .unsqueeze(1)
+                        .to_broadcast([P, 32, TPB, 4]),
+                        op=ADD,
+                    )
+                    nc.scalar.copy(
+                        out=inxw[:, :, TPB * b : TPB * (b + 1), :],
+                        in_=xtp[:].bitcast(F32).rearrange("p (s c u) -> p c s u", s=TPB, c=32, u=2),
+                    )
+                if 1 <= n <= NG:
+                    quantise(n - 1, b)
+                if n + 1 < NG:
+                    perm_w(n + 1, b)
+                if b == 1 and 2 <= n <= NG:
+                    first_products(n - 2, "ssss")
+                if b == 2 and n + XG < NG:
+                    perm_x(n + XG, "s")
+                if b == 3:
+                    if n == 2:
+                        prepare_b3()
+                    if 3 <= n < 7:
+                        prepare_w3(n - 3)
+            if n == 7:
+                nc.vector.quantize_mx(out=w3c[:].bitcast(FP8X4), scales=w3s[:], in_=inw3[:])
+
+        first_products(NG - 1, "vsvs")
+        banks = [(psw, "wtp"), (psx, "xtp"), (psz, "zp")]
+        inz = const.tile([P, 4096], BF16, name="inz", align_bytes=64)
+        inzv = inz[:].rearrange("p (t i c) -> p t i c", t=32, i=32, c=4)
+        zts = []
+        for b in range(8):
+            pool, tag = banks[b % 3]
+            zt = pool.tile([P, 512], F32, name="zt", tag=tag)
+            for s in range(4):
+                i = 4 * b + s
+                nc.tensor.transpose(zt[:, s * P : (s + 1) * P], zc[:, i * P : (i + 1) * P], ident_f[:])
+            zts.append(zt)
+        zq = const.tile([P, 1024], U32, name="zq", align_bytes=64)
+        zs = const.tile([P, 1024], U8, name="zs", align_bytes=64)
+        for h in range(2):
+            for b in range(8):
+                src = zts[b][:].rearrange("p (s c t) -> p t s c", s=4, c=4, t=32)[:, 16 * h : 16 * h + 16, :, :]
+                dst = inzv[:, 16 * h : 16 * h + 16, 4 * b : 4 * b + 4, :]
+                if b % 2 == 0:
+                    nc.vector.tensor_copy(out=dst, in_=src)
+                else:
+                    nc.scalar.copy(out=dst, in_=src)
+            nc.vector.quantize_mx(
+                out=zq[:, 512 * h : 512 * (h + 1)].bitcast(FP8X4),
+                scales=zs[:, 512 * h : 512 * (h + 1)],
+                in_=inz[:, 2048 * h : 2048 * (h + 1)],
+            )
+        k = 0
+        for h in range(2):
+            for ot in range(8):
+                pool, tag = banks[k % 3]
+                yp = pool.tile([P, 512], F32, name="yp", tag=tag)
+                nc.tensor.matmul_mx(
+                    out=yp[:],
+                    lhsT=w3c[:, ot * P : (ot + 1) * P].bitcast(FP8X4),
+                    lhsT_scale=w3s[:, ot * P : (ot + 1) * P],
+                    rhs=zq[:, h * 512 : (h + 1) * 512].bitcast(FP8X4),
+                    rhs_scale=zs[:, h * 512 : (h + 1) * 512],
+                    start=True,
+                    stop=True,
+                )
+                y = ypool.tile([P, 512], F32, name="y")
+                if k % 2 == 0:
+                    nc.vector.tensor_scalar_add(out=y[:], in0=yp[:], scalar1=b3f[:, ot : ot + 1])
+                else:
+                    nc.scalar.activation(out=y[:], in_=yp[:], func=IDENTITY, bias=b3f[:, ot : ot + 1], scale=1.0)
+                nc.sync.dma_start(out=outv[:, ot, h * 512 : (h + 1) * 512], in_=y[:])
+                k += 1

@@ -18,7 +18,7 @@ NG = 16
 XG = 4
 FR = 35
 XE = FR * 32
-TPB = 8
+TPB = 4
 NB = 32 // TPB
 
 
@@ -218,15 +218,15 @@ def tile_gccgc_pa_kernel(tc, x_pad, rel, A, w3, b3, out):
                         out=inxw[:, :, TPB * b : TPB * (b + 1), :],
                         in_=xtp[:].bitcast(F32).rearrange("p (s c u) -> p c s u", s=TPB, c=32, u=2),
                     )
-                if 1 <= n <= NG:
-                    quantise(n - 1, b)
-                if n + 1 < NG:
-                    perm_w(n + 1, b)
-                if b == 1 and 2 <= n <= NG:
+                if 1 <= n <= NG and b % 2 == 0:
+                    quantise(n - 1, b // 2)
+                if n + 1 < NG and b % 2 == 1:
+                    perm_w(n + 1, b // 2)
+                if b == 2 and 2 <= n <= NG:
                     first_products(n - 2, "ssss")
-                if b == 2 and n + XG < NG:
+                if b == 4 and n + XG < NG:
                     perm_x(n + XG, "s")
-                if b == 3:
+                if b == 6:
                     if n == 2:
                         prepare_b3()
                     if 3 <= n < 7:

@@ -37,8 +37,9 @@ def tile_gccgc_pa_kernel(tc, x_pad, rel, A, w3, b3, out):
         work = ctx.enter_context(tc.tile_pool(name="work", bufs=2))
         ypool = ctx.enter_context(tc.tile_pool(name="ypool", bufs=4))
         psw = ctx.enter_context(tc.psum_pool(name="psw", bufs=3))
-        psx = ctx.enter_context(tc.psum_pool(name="psx", bufs=3))
+        psx = ctx.enter_context(tc.psum_pool(name="psx", bufs=2))
         psz = ctx.enter_context(tc.psum_pool(name="psz", bufs=2))
+        psj = ctx.enter_context(tc.psum_pool(name="psj", bufs=1))
 
         r_t, pn_t, xt_t, xp_t = {}, {}, {}, {}
         inw_t, inx_t, q_t = {}, {}, {}
@@ -74,6 +75,25 @@ def tile_gccgc_pa_kernel(tc, x_pad, rel, A, w3, b3, out):
                 out=pn_t[n][:].bitcast(F32).rearrange("p (w q m a) -> p q m w a", w=16, q=4, m=8, a=4)[:, kq],
                 in_=r_t[n][:].bitcast(F32).rearrange("p (q a m w) -> p q m w a", q=4, a=4, m=8, w=16)[:, kq],
             )
+
+        ones = const.tile([P, 2048], BF16, name="ones", align_bytes=64)
+        nc.vector.memset(ones[:], 1.0)
+        onec = const.tile([P, 512], U32, name="onec", align_bytes=64)
+        ones_s = const.tile([P, 512], U8, name="ones_s", align_bytes=64)
+        nc.vector.quantize_mx(out=onec[:].bitcast(FP8X4), scales=ones_s[:], in_=ones[:])
+        junk = psj.tile([P, 512], F32, name="junk")
+
+        def kick():
+            for rep in range(2):
+                nc.tensor.matmul_mx(
+                    out=junk[:],
+                    lhsT=onec[:, 0:P].bitcast(FP8X4),
+                    lhsT_scale=ones_s[:, 0:P],
+                    rhs=onec[:].bitcast(FP8X4),
+                    rhs_scale=ones_s[:],
+                    start=True,
+                    stop=True,
+                )
 
         az = const.tile([P, P], BF16, name="az")
         nc.vector.memset(az[:], 0.0)
@@ -136,21 +156,26 @@ def tile_gccgc_pa_kernel(tc, x_pad, rel, A, w3, b3, out):
                 in_=w3p[:].rearrange("p (t u o) -> p t o u", t=2, u=2, o=P),
             )
 
-        def first_products(n, engines):
+        zp_t = {}
+
+        def first_products(n, q, engines):
             xc, xs, wc, ws = q_t[n]
-            for hb in range(2):
-                zp = psz.tile([P, 512], F32, name="zp")
-                for s in range(4):
-                    cols = slice((4 * hb + s) * P, (4 * hb + s + 1) * P)
-                    nc.tensor.matmul_mx(
-                        out=zp[:, s * P : (s + 1) * P],
-                        lhsT=xc[:, cols].bitcast(FP8X4),
-                        lhsT_scale=xs[:, cols],
-                        rhs=wc[:, cols].bitcast(FP8X4),
-                        rhs_scale=ws[:, cols],
-                        start=True,
-                        stop=True,
-                    )
+            hb = q // 2
+            if q % 2 == 0:
+                zp_t[hb] = psz.tile([P, 512], F32, name="zp")
+            zp = zp_t[hb]
+            for s in (2 * (q % 2), 2 * (q % 2) + 1):
+                cols = slice((4 * hb + s) * P, (4 * hb + s + 1) * P)
+                nc.tensor.matmul_mx(
+                    out=zp[:, s * P : (s + 1) * P],
+                    lhsT=xc[:, cols].bitcast(FP8X4),
+                    lhsT_scale=xs[:, cols],
+                    rhs=wc[:, cols].bitcast(FP8X4),
+                    rhs_scale=ws[:, cols],
+                    start=True,
+                    stop=True,
+                )
+            if q % 2 == 1:
                 g0 = 8 * n + 4 * hb
                 for c4 in range(4):
                     rows = slice(32 * c4, 32 * c4 + 32)
@@ -222,8 +247,11 @@ def tile_gccgc_pa_kernel(tc, x_pad, rel, A, w3, b3, out):
                     quantise(n - 1, b // 2)
                 if n + 1 < NG and b % 2 == 1:
                     perm_w(n + 1, b // 2)
-                if b == 2 and 2 <= n <= NG:
-                    first_products(n - 2, "ssss")
+                if b % 2 == 1:
+                    if 2 <= n:
+                        first_products(n - 2, b // 2, "ssss")
+                    if b == 1 and n < NG:
+                        kick()
                 if b == 4 and n + XG < NG:
                     perm_x(n + XG, "s")
                 if b == 6:
@@ -234,13 +262,14 @@ def tile_gccgc_pa_kernel(tc, x_pad, rel, A, w3, b3, out):
             if n == 7:
                 nc.vector.quantize_mx(out=w3c[:].bitcast(FP8X4), scales=w3s[:], in_=inw3[:])
 
-        first_products(NG - 1, "vsvs")
-        banks = [(psw, "wtp"), (psx, "xtp"), (psz, "zp")]
+        for q in range(4):
+            first_products(NG - 1, q, "vsvs")
+        banks = [(psw, "wtp"), (psx, "xtp"), (psz, "zp"), (psw, "wtp"), (psx, "xtp"), (psz, "zp"), (psw, "wtp"), (psj, "junk")]
         inz = const.tile([P, 4096], BF16, name="inz", align_bytes=64)
         inzv = inz[:].rearrange("p (t i c) -> p t i c", t=32, i=32, c=4)
         zts = []
         for b in range(8):
-            pool, tag = banks[b % 3]
+            pool, tag = banks[b]
             zt = pool.tile([P, 512], F32, name="zt", tag=tag)
             for s in range(4):
                 i = 4 * b + s
@@ -264,7 +293,7 @@ def tile_gccgc_pa_kernel(tc, x_pad, rel, A, w3, b3, out):
         k = 0
         for h in range(2):
             for ot in range(8):
-                pool, tag = banks[k % 3]
+                pool, tag = banks[k % 8]
                 yp = pool.tile([P, 512], F32, name="yp", tag=tag)
                 nc.tensor.matmul_mx(
                     out=yp[:],

@@ -20,6 +20,7 @@ FR = 35
 XE = FR * 32
 TPB = 4
 NB = 32 // TPB
+KICKS = (2, 1, 1, 1)
 
 
 def tile_gccgc_pa_kernel(tc, x_pad, rel, A, w3, b3, out):
@@ -76,6 +77,17 @@ def tile_gccgc_pa_kernel(tc, x_pad, rel, A, w3, b3, out):
                 in_=r_t[n][:].bitcast(F32).rearrange("p (q a m w) -> p q m w a", q=4, a=4, m=8, w=16)[:, kq],
             )
 
+        az = const.tile([P, P], BF16, name="az")
+        nc.vector.memset(az[:], 0.0)
+        bz = const.tile([P, P], BF16, name="bz")
+        nc.vector.memset(bz[:], 0.0)
+        load_x(0)
+        load_rel(0)
+        nc.sync.dma_start(out=az[0:32, 0:32], in_=A)
+        load_rel(1)
+        load_x(1)
+        nc.sync.dma_start(out=bz[0:8, :], in_=b3v)
+
         ones = const.tile([P, 2048], BF16, name="ones", align_bytes=64)
         nc.vector.memset(ones[:], 1.0)
         onec = const.tile([P, 512], U32, name="onec", align_bytes=64)
@@ -83,8 +95,8 @@ def tile_gccgc_pa_kernel(tc, x_pad, rel, A, w3, b3, out):
         nc.vector.quantize_mx(out=onec[:].bitcast(FP8X4), scales=ones_s[:], in_=ones[:])
         junk = psj.tile([P, 512], F32, name="junk")
 
-        def kick():
-            for rep in range(2):
+        def kick(times):
+            for rep in range(times):
                 nc.tensor.matmul_mx(
                     out=junk[:],
                     lhsT=onec[:, 0:P].bitcast(FP8X4),
@@ -94,17 +106,6 @@ def tile_gccgc_pa_kernel(tc, x_pad, rel, A, w3, b3, out):
                     start=True,
                     stop=True,
                 )
-
-        az = const.tile([P, P], BF16, name="az")
-        nc.vector.memset(az[:], 0.0)
-        bz = const.tile([P, P], BF16, name="bz")
-        nc.vector.memset(bz[:], 0.0)
-        nc.sync.dma_start(out=az[0:32, 0:32], in_=A)
-        load_x(0)
-        load_rel(0)
-        load_rel(1)
-        load_x(1)
-        nc.sync.dma_start(out=bz[0:8, :], in_=b3v)
 
         ident_b = const.tile([P, P], BF16, name="ident_b")
         make_identity(nc, ident_b[:])
@@ -250,8 +251,8 @@ def tile_gccgc_pa_kernel(tc, x_pad, rel, A, w3, b3, out):
                 if b % 2 == 1:
                     if 2 <= n:
                         first_products(n - 2, b // 2, "ssss")
-                    if b == 1 and n < NG:
-                        kick()
+                    if n < NG:
+                        kick(KICKS[b // 2])
                 if b == 4 and n + XG < NG:
                     perm_x(n + XG, "s")
                 if b == 6:

@@ -250,11 +250,11 @@ def tile_gccgc_pa_kernel(tc, x_pad, rel, A, w3, b3, out):
                     perm_w(n + 1, b // 2)
                 if b % 2 == 1:
                     if 2 <= n:
-                        first_products(n - 2, b // 2, "ssss")
+                        first_products(n - 2, b // 2, "vvvv")
                     if n < NG:
                         kick(KICKS[b // 2])
                 if b == 4 and n + XG < NG:
-                    perm_x(n + XG, "s")
+                    perm_x(n + XG, "v")
                 if b == 6:
                     if n == 2:
                         prepare_b3()

@@ -121,13 +121,11 @@ def tile_gccgc_pa_kernel(tc, x_pad, rel, A, w3, b3, out):
         )
         ps2 = psz.tile([P, P], BF16, name="ps2", tag="zp")
         nc.tensor.transpose(ps2[:], atr[:], ident_b[:])
-        arep = const.tile([P, P], BF16, name="arep")
+        arep = const.tile([P, 512], BF16, name="arep")
         nc.vector.tensor_copy(
-            out=arep[:].rearrange("p (i t) -> p i t", t=4),
-            in_=ps2[:, 0:32].unsqueeze(2).to_broadcast([P, 32, 4]),
+            out=arep[:].rearrange("p (i e) -> p i e", e=16),
+            in_=ps2[:, 0:32].unsqueeze(2).to_broadcast([P, 32, 16]),
         )
-        acol = const.tile([P, 32], F32, name="acol")
-        nc.vector.tensor_copy(out=acol[:], in_=ps2[:, 0:32])
 
         for n in range(XG):
             perm_x(n, "v")
@@ -181,7 +179,7 @@ def tile_gccgc_pa_kernel(tc, x_pad, rel, A, w3, b3, out):
                 for c4 in range(4):
                     rows = slice(32 * c4, 32 * c4 + 32)
                     dst = zcv[rows, :, g0 : g0 + 4]
-                    src = zp[rows, :].rearrange("p (g c i) -> p c i g", g=4, c=4, i=32)[:, c4, :, :]
+                    src = zp[rows, :].rearrange("p (g i c) -> p c i g", g=4, c=4, i=32)[:, c4, :, :]
                     if engines[c4] == "v":
                         nc.vector.tensor_copy(out=dst, in_=src)
                     else:
@@ -216,7 +214,7 @@ def tile_gccgc_pa_kernel(tc, x_pad, rel, A, w3, b3, out):
                 xp = xp_t[n // XG]
                 x0 = (n % XG) * XE
                 inw_t[n] = work.tile([P, 4096], BF16, name="inw", align_bytes=64)
-                inwv = inw_t[n][:].rearrange("p (c i t) -> p c i t", c=32, i=32, t=4)
+                inwv = inw_t[n][:].rearrange("p (g i e) -> p g i e", g=8, i=32, e=16)
                 inx_t[n] = work.tile([P, 4096], BF16, name="inx", align_bytes=64)
                 inxw = inx_t[n][:].bitcast(F32).rearrange("p (c t u) -> p c t u", c=32, t=32, u=2)
             for b in range(NB):
@@ -224,25 +222,31 @@ def tile_gccgc_pa_kernel(tc, x_pad, rel, A, w3, b3, out):
                     wtp = psw.tile([P, TPB * P], BF16, name="wtp")
                     for s in range(TPB):
                         i = TPB * b + s
-                        nc.tensor.transpose(wtp[:, s * P : (s + 1) * P], pv[:, i // 2, :, i % 2], ident_b[:])
+                        nc.tensor.transpose(
+                            wtp[:].rearrange("p (g s e) -> p s g e", g=8, s=TPB, e=16)[:, s],
+                            pv[:, i // 2, :, i % 2],
+                            ident_b[:],
+                        )
                     xtp = psx.tile([P, TPB * P], BF16, name="xtp")
                     for s in range(TPB):
                         t = TPB * b + s
                         nc.tensor.transpose(
-                            xtp[:, s * P : (s + 1) * P], xp[:, x0 + 32 * t : x0 + 32 * t + P], ident_b[:]
+                            xtp[:].rearrange("p (c s t) -> p s c t", c=32, s=TPB, t=4)[:, s],
+                            xp[:, x0 + 32 * t : x0 + 32 * t + P],
+                            ident_b[:],
                         )
                     nc.vector.tensor_tensor(
                         out=inwv[:, :, TPB * b : TPB * (b + 1), :],
-                        in0=wtp[:].rearrange("p (s c t) -> p c s t", s=TPB, c=32, t=4),
-                        in1=arep[:, 4 * TPB * b : 4 * TPB * (b + 1)]
-                        .rearrange("p (s t) -> p s t", t=4)
+                        in0=wtp[:].rearrange("p (g s e) -> p g s e", g=8, s=TPB, e=16),
+                        in1=arep[:, 16 * TPB * b : 16 * TPB * (b + 1)]
+                        .rearrange("p (s e) -> p s e", e=16)
                         .unsqueeze(1)
-                        .to_broadcast([P, 32, TPB, 4]),
+                        .to_broadcast([P, 8, TPB, 16]),
                         op=ADD,
                     )
                     nc.scalar.copy(
                         out=inxw[:, :, TPB * b : TPB * (b + 1), :],
-                        in_=xtp[:].bitcast(F32).rearrange("p (s c u) -> p c s u", s=TPB, c=32, u=2),
+                        in_=xtp[:].bitcast(F32).rearrange("p (c s u) -> p c s u", s=TPB, c=32, u=2),
                     )
                 if 1 <= n <= NG and b % 2 == 0:
                     quantise(n - 1, b // 2)
@@ -250,11 +254,11 @@ def tile_gccgc_pa_kernel(tc, x_pad, rel, A, w3, b3, out):
                     perm_w(n + 1, b // 2)
                 if b % 2 == 1:
                     if 2 <= n:
-                        first_products(n - 2, b // 2, "vvvv")
+                        first_products(n - 2, b // 2, "ssss")
                     if n < NG:
                         kick(KICKS[b // 2])
                 if b == 4 and n + XG < NG:
-                    perm_x(n + XG, "v")
+                    perm_x(n + XG, "s")
                 if b == 6:
                     if n == 2:
                         prepare_b3()

@@ -121,11 +121,8 @@ def tile_gccgc_pa_kernel(tc, x_pad, rel, A, w3, b3, out):
         )
         ps2 = psz.tile([P, P], BF16, name="ps2", tag="zp")
         nc.tensor.transpose(ps2[:], atr[:], ident_b[:])
-        arep = const.tile([P, 512], BF16, name="arep")
-        nc.vector.tensor_copy(
-            out=arep[:].rearrange("p (i e) -> p i e", e=16),
-            in_=ps2[:, 0:32].unsqueeze(2).to_broadcast([P, 32, 16]),
-        )
+        acol = const.tile([P, 32], F32, name="acol")
+        nc.vector.tensor_copy(out=acol[:], in_=ps2[:, 0:32])
 
         for n in range(XG):
             perm_x(n, "v")
@@ -222,11 +219,7 @@ def tile_gccgc_pa_kernel(tc, x_pad, rel, A, w3, b3, out):
                     wtp = psw.tile([P, TPB * P], BF16, name="wtp")
                     for s in range(TPB):
                         i = TPB * b + s
-                        nc.tensor.transpose(
-                            wtp[:].rearrange("p (g s e) -> p s g e", g=8, s=TPB, e=16)[:, s],
-                            pv[:, i // 2, :, i % 2],
-                            ident_b[:],
-                        )
+                        nc.tensor.transpose(wtp[:, s * P : (s + 1) * P], pv[:, i // 2, :, i % 2], ident_b[:])
                     xtp = psx.tile([P, TPB * P], BF16, name="xtp")
                     for s in range(TPB):
                         t = TPB * b + s
@@ -235,15 +228,13 @@ def tile_gccgc_pa_kernel(tc, x_pad, rel, A, w3, b3, out):
                             xp[:, x0 + 32 * t : x0 + 32 * t + P],
                             ident_b[:],
                         )
-                    nc.vector.tensor_tensor(
-                        out=inwv[:, :, TPB * b : TPB * (b + 1), :],
-                        in0=wtp[:].rearrange("p (g s e) -> p g s e", g=8, s=TPB, e=16),
-                        in1=arep[:, 16 * TPB * b : 16 * TPB * (b + 1)]
-                        .rearrange("p (s e) -> p s e", e=16)
-                        .unsqueeze(1)
-                        .to_broadcast([P, 8, TPB, 16]),
-                        op=ADD,
-                    )
+                    for s in range(TPB):
+                        i = TPB * b + s
+                        nc.vector.tensor_scalar_add(
+                            out=inwv[:, :, i, :],
+                            in0=wtp[:, s * P : (s + 1) * P].rearrange("p (g e) -> p g e", e=16),
+                            scalar1=acol[:, i : i + 1],
+                        )
                     nc.scalar.copy(
                         out=inxw[:, :, TPB * b : TPB * (b + 1), :],
                         in_=xtp[:].bitcast(F32).rearrange("p (c s u) -> p c s u", s=TPB, c=32, u=2),

@@ -50,15 +50,15 @@ def tile_gccgc_pa_kernel(tc, x_pad, rel, A, w3, b3, out):
             nc.sync.dma_start(out=r[:], in_=relv[:, n, :])
             r_t[n] = r
 
-        def load_x(k):
-            xt = work.tile([P, XG * XE], BF16, name="xt")
-            xtv = xt[:].rearrange("p (n e) -> p n e", n=XG)
+        def load_x(k, lo, hi):
+            if lo == 0:
+                xt_t[k] = work.tile([P, XG * XE], BF16, name="xt")
+                xp_t[k] = work.tile([P, XG * XE], BF16, name="xp")
+            xtv = xt_t[k][:].rearrange("p (n e) -> p n e", n=XG)
             for tt in range(4):
                 nc.sync.dma_start(
-                    out=xtv[tt:P:4, :, :], in_=xv[:, XG * k : XG * (k + 1), 128 * tt : 128 * tt + XE]
+                    out=xtv[tt:P:4, lo:hi, :], in_=xv[:, XG * k + lo : XG * k + hi, 128 * tt : 128 * tt + XE]
                 )
-            xt_t[k] = xt
-            xp_t[k] = work.tile([P, XG * XE], BF16, name="xp")
 
         def perm_x(n, eng):
             k, e0 = n // XG, (n % XG) * XE
@@ -81,11 +81,12 @@ def tile_gccgc_pa_kernel(tc, x_pad, rel, A, w3, b3, out):
         nc.vector.memset(az[:], 0.0)
         bz = const.tile([P, P], BF16, name="bz")
         nc.vector.memset(bz[:], 0.0)
-        load_x(0)
-        load_rel(0)
         nc.sync.dma_start(out=az[0:32, 0:32], in_=A)
+        load_x(0, 0, 1)
+        load_rel(0)
+        load_x(0, 1, XG)
         load_rel(1)
-        load_x(1)
+        load_x(1, 0, XG)
         nc.sync.dma_start(out=bz[0:8, :], in_=b3v)
 
         ones = const.tile([P, 2048], BF16, name="ones", align_bytes=64)
@@ -121,15 +122,23 @@ def tile_gccgc_pa_kernel(tc, x_pad, rel, A, w3, b3, out):
         )
         ps2 = psz.tile([P, P], BF16, name="ps2", tag="zp")
         nc.tensor.transpose(ps2[:], atr[:], ident_b[:])
+        arep = const.tile([P, P], BF16, name="arep")
+        nc.vector.tensor_copy(
+            out=arep[:].rearrange("p (i t) -> p i t", t=4),
+            in_=ps2[:, 0:32].unsqueeze(2).to_broadcast([P, 32, 4]),
+        )
         acol = const.tile([P, 32], F32, name="acol")
         nc.vector.tensor_copy(out=acol[:], in_=ps2[:, 0:32])
 
-        for n in range(XG):
-            perm_x(n, "v")
-            perm_w(0, n)
+        perm_x(0, "v")
+        for kq in range(4):
+            perm_w(0, kq)
+        for n in range(1, XG):
+            perm_x(n, "s")
 
-        zc = const.tile([P, 4096], F32, name="zc")
+        zc = const.tile([P, 4096], BF16, name="zc")
         zcv = zc[:].rearrange("p (i g) -> p i g", g=P)
+        zs_t = {}
         b3f = const.tile([P, 8], F32, name="b3f")
         w3c = const.tile([P, 1024], U32, name="w3c", align_bytes=64)
         w3s = const.tile([P, 1024], U8, name="w3s", align_bytes=64)
@@ -154,7 +163,7 @@ def tile_gccgc_pa_kernel(tc, x_pad, rel, A, w3, b3, out):
 
         zp_t = {}
 
-        def first_products(n, q, engines):
+        def first_products(n, q):
             xc, xs, wc, ws = q_t[n]
             hb = q // 2
             if q % 2 == 0:
@@ -172,15 +181,21 @@ def tile_gccgc_pa_kernel(tc, x_pad, rel, A, w3, b3, out):
                     stop=True,
                 )
             if q % 2 == 1:
-                g0 = 8 * n + 4 * hb
+                if n % 4 == 0 and hb == 0:
+                    zs_t[n // 4] = work.tile([P, 4096], BF16, name="zs")
+                zsv = zs_t[n // 4][:].rearrange("p (c i g) -> p c i g", c=4, i=32, g=32)
+                g0 = 8 * (n % 4) + 4 * hb
                 for c4 in range(4):
-                    rows = slice(32 * c4, 32 * c4 + 32)
-                    dst = zcv[rows, :, g0 : g0 + 4]
-                    src = zp[rows, :].rearrange("p (g i c) -> p c i g", g=4, c=4, i=32)[:, c4, :, :]
-                    if engines[c4] == "v":
-                        nc.vector.tensor_copy(out=dst, in_=src)
-                    else:
-                        nc.scalar.copy(out=dst, in_=src)
+                    nc.scalar.copy(
+                        out=zsv[:, c4, :, g0 : g0 + 4],
+                        in_=zp[:].rearrange("p (g c i) -> p c i g", g=4, c=4, i=32)[:, c4, :, :],
+                    )
+
+        def merge_z(k):
+            zsv = zs_t[k][:].rearrange("p (c i g) -> p c i g", c=4, i=32, g=32)
+            for c4 in (1, 2, 3, 0):
+                rows = slice(32 * c4, 32 * c4 + 32)
+                nc.vector.tensor_copy(out=zcv[rows, :, 32 * k : 32 * (k + 1)], in_=zsv[rows, c4, :, :])
 
         def quantise(n, piece):
             if piece == 0:
@@ -203,7 +218,7 @@ def tile_gccgc_pa_kernel(tc, x_pad, rel, A, w3, b3, out):
             if n + 2 < NG:
                 load_rel(n + 2)
             if n % XG == XG - 1 and n // XG + 2 < NG // XG:
-                load_x(n // XG + 2)
+                load_x(n // XG + 2, 0, XG)
             if n == 1:
                 nc.sync.dma_start(out=w3r[:].rearrange("p (t c) -> p t c", t=8), in_=w3v)
             if n < NG:
@@ -211,7 +226,7 @@ def tile_gccgc_pa_kernel(tc, x_pad, rel, A, w3, b3, out):
                 xp = xp_t[n // XG]
                 x0 = (n % XG) * XE
                 inw_t[n] = work.tile([P, 4096], BF16, name="inw", align_bytes=64)
-                inwv = inw_t[n][:].rearrange("p (g i e) -> p g i e", g=8, i=32, e=16)
+                inwv = inw_t[n][:].rearrange("p (c i t) -> p c i t", c=32, i=32, t=4)
                 inx_t[n] = work.tile([P, 4096], BF16, name="inx", align_bytes=64)
                 inxw = inx_t[n][:].bitcast(F32).rearrange("p (c t u) -> p c t u", c=32, t=32, u=2)
             for b in range(NB):
@@ -224,20 +239,20 @@ def tile_gccgc_pa_kernel(tc, x_pad, rel, A, w3, b3, out):
                     for s in range(TPB):
                         t = TPB * b + s
                         nc.tensor.transpose(
-                            xtp[:].rearrange("p (c s t) -> p s c t", c=32, s=TPB, t=4)[:, s],
-                            xp[:, x0 + 32 * t : x0 + 32 * t + P],
-                            ident_b[:],
+                            xtp[:, s * P : (s + 1) * P], xp[:, x0 + 32 * t : x0 + 32 * t + P], ident_b[:]
                         )
-                    for s in range(TPB):
-                        i = TPB * b + s
-                        nc.vector.tensor_scalar_add(
-                            out=inwv[:, :, i, :],
-                            in0=wtp[:, s * P : (s + 1) * P].rearrange("p (g e) -> p g e", e=16),
-                            scalar1=acol[:, i : i + 1],
-                        )
+                    nc.vector.tensor_tensor(
+                        out=inwv[:, :, TPB * b : TPB * (b + 1), :],
+                        in0=wtp[:].rearrange("p (s c t) -> p c s t", s=TPB, c=32, t=4),
+                        in1=arep[:, 4 * TPB * b : 4 * TPB * (b + 1)]
+                        .rearrange("p (s t) -> p s t", t=4)
+                        .unsqueeze(1)
+                        .to_broadcast([P, 32, TPB, 4]),
+                        op=ADD,
+                    )
                     nc.scalar.copy(
                         out=inxw[:, :, TPB * b : TPB * (b + 1), :],
-                        in_=xtp[:].bitcast(F32).rearrange("p (c s u) -> p c s u", s=TPB, c=32, u=2),
+                        in_=xtp[:].bitcast(F32).rearrange("p (s c u) -> p c s u", s=TPB, c=32, u=2),
                     )
                 if 1 <= n <= NG and b % 2 == 0:
                     quantise(n - 1, b // 2)
@@ -245,9 +260,11 @@ def tile_gccgc_pa_kernel(tc, x_pad, rel, A, w3, b3, out):
                     perm_w(n + 1, b // 2)
                 if b % 2 == 1:
                     if 2 <= n:
-                        first_products(n - 2, b // 2, "ssss")
+                        first_products(n - 2, b // 2)
                     if n < NG:
                         kick(KICKS[b // 2])
+                if b == 2 and n >= 6 and n % 4 == 2:
+                    merge_z((n - 6) // 4)
                 if b == 4 and n + XG < NG:
                     perm_x(n + XG, "s")
                 if b == 6:
@@ -259,17 +276,18 @@ def tile_gccgc_pa_kernel(tc, x_pad, rel, A, w3, b3, out):
                 nc.vector.quantize_mx(out=w3c[:].bitcast(FP8X4), scales=w3s[:], in_=inw3[:])
 
         for q in range(4):
-            first_products(NG - 1, q, "vsvs")
+            first_products(NG - 1, q)
+        merge_z(3)
         banks = [(psw, "wtp"), (psx, "xtp"), (psz, "zp"), (psw, "wtp"), (psx, "xtp"), (psz, "zp"), (psw, "wtp"), (psj, "junk")]
         inz = const.tile([P, 4096], BF16, name="inz", align_bytes=64)
         inzv = inz[:].rearrange("p (t i c) -> p t i c", t=32, i=32, c=4)
         zts = []
         for b in range(8):
             pool, tag = banks[b]
-            zt = pool.tile([P, 512], F32, name="zt", tag=tag)
+            zt = pool.tile([P, 512], BF16, name="zt", tag=tag)
             for s in range(4):
                 i = 4 * b + s
-                nc.tensor.transpose(zt[:, s * P : (s + 1) * P], zc[:, i * P : (i + 1) * P], ident_f[:])
+                nc.tensor.transpose(zt[:, s * P : (s + 1) * P], zc[:, i * P : (i + 1) * P], ident_b[:])
             zts.append(zt)
         zq = const.tile([P, 1024], U32, name="zq", align_bytes=64)
         zs = const.tile([P, 1024], U8, name="zs", align_bytes=64)

@@ -62,8 +62,8 @@ def tile_gccgc_pa_kernel(tc, x_pad, rel, A, w3, b3, out):
 
         def perm_x(n, eng):
             k, e0 = n // XG, (n % XG) * XE
-            dst = xp_t[k][:, e0 : e0 + XE].rearrange("p (f m a) -> p f m a", m=8, a=4)
-            src = xt_t[k][:, e0 : e0 + XE].rearrange("p (f a m) -> p f m a", m=8, a=4)
+            dst = xp_t[k][:, e0 : e0 + XE].rearrange("p (f m e a) -> p f m a e", m=2, e=4, a=4)
+            src = xt_t[k][:, e0 : e0 + XE].rearrange("p (f a m e) -> p f m a e", m=2, e=4, a=4)
             if eng == "v":
                 nc.vector.tensor_copy(out=dst, in_=src)
             else:
@@ -73,8 +73,8 @@ def tile_gccgc_pa_kernel(tc, x_pad, rel, A, w3, b3, out):
             if kq == 0:
                 pn_t[n] = work.tile([P, 4096], BF16, name="pn")
             nc.vector.tensor_copy(
-                out=pn_t[n][:].bitcast(F32).rearrange("p (w q m a) -> p q m w a", w=16, q=4, m=8, a=4)[:, kq],
-                in_=r_t[n][:].bitcast(F32).rearrange("p (q a m w) -> p q m w a", q=4, a=4, m=8, w=16)[:, kq],
+                out=pn_t[n][:].bitcast(F32).rearrange("p (w v q m a) -> p q m w a v", w=8, v=2, q=4, m=8, a=4)[:, kq],
+                in_=r_t[n][:].bitcast(F32).rearrange("p (q a m w v) -> p q m w a v", q=4, a=4, m=8, w=8, v=2)[:, kq],
             )
 
         az = const.tile([P, P], BF16, name="az")

@@ -69,13 +69,15 @@ def tile_gccgc_pa_kernel(tc, x_pad, rel, A, w3, b3, out):
             else:
                 nc.scalar.copy(out=dst, in_=src)
 
-        def perm_w(n, kq):
-            if kq == 0:
+        def perm_w(n, b, eng):
+            if b == 0:
                 pn_t[n] = work.tile([P, 4096], BF16, name="pn")
-            nc.vector.tensor_copy(
-                out=pn_t[n][:].bitcast(F32).rearrange("p (w v q m a) -> p q m w a v", w=8, v=2, q=4, m=8, a=4)[:, kq],
-                in_=r_t[n][:].bitcast(F32).rearrange("p (q a m w v) -> p q m w a v", q=4, a=4, m=8, w=8, v=2)[:, kq],
-            )
+            dst = pn_t[n][:].rearrange("p (i v q m a) -> p i q m a v", i=8, v=4, q=4, m=8, a=4)[:, b]
+            src = r_t[n][:].rearrange("p (q a m i v) -> p i q m a v", q=4, a=4, m=8, i=8, v=4)[:, b]
+            if eng == "v":
+                nc.vector.tensor_copy(out=dst, in_=src)
+            else:
+                nc.scalar.copy(out=dst, in_=src)
 
         az = const.tile([P, P], BF16, name="az")
         nc.vector.memset(az[:], 0.0)
@@ -131,8 +133,8 @@ def tile_gccgc_pa_kernel(tc, x_pad, rel, A, w3, b3, out):
         nc.vector.tensor_copy(out=acol[:], in_=ps2[:, 0:32])
 
         perm_x(0, "v")
-        for kq in range(4):
-            perm_w(0, kq)
+        for b in range(NB):
+            perm_w(0, b, "v")
         for n in range(1, XG):
             perm_x(n, "s")
 
@@ -222,7 +224,7 @@ def tile_gccgc_pa_kernel(tc, x_pad, rel, A, w3, b3, out):
             if n == 1:
                 nc.sync.dma_start(out=w3r[:].rearrange("p (t c) -> p t c", t=8), in_=w3v)
             if n < NG:
-                pv = pn_t[n][:].rearrange("p (w q h) -> p w q h", w=16, q=P, h=2)
+                pv = pn_t[n][:].rearrange("p (i k) -> p i k", i=32)
                 xp = xp_t[n // XG]
                 x0 = (n % XG) * XE
                 inw_t[n] = work.tile([P, 4096], BF16, name="inw", align_bytes=64)
@@ -234,7 +236,7 @@ def tile_gccgc_pa_kernel(tc, x_pad, rel, A, w3, b3, out):
                     wtp = psw.tile([P, TPB * P], BF16, name="wtp")
                     for s in range(TPB):
                         i = TPB * b + s
-                        nc.tensor.transpose(wtp[:, s * P : (s + 1) * P], pv[:, i // 2, :, i % 2], ident_b[:])
+                        nc.tensor.transpose(wtp[:, s * P : (s + 1) * P], pv[:, i, :], ident_b[:])
                     xtp = psx.tile([P, TPB * P], BF16, name="xtp")
                     for s in range(TPB):
                         t = TPB * b + s
@@ -256,8 +258,8 @@ def tile_gccgc_pa_kernel(tc, x_pad, rel, A, w3, b3, out):
                     )
                 if 1 <= n <= NG and b % 2 == 0:
                     quantise(n - 1, b // 2)
-                if n + 1 < NG and b % 2 == 1:
-                    perm_w(n + 1, b // 2)
+                if n + 1 < NG:
+                    perm_w(n + 1, b, "s" if b in (2, 6) else "v")
                 if b % 2 == 1:
                     if 2 <= n:
                         first_products(n - 2, b // 2)

@@ -20,7 +20,7 @@ FR = 35
 XE = FR * 32
 TPB = 4
 NB = 32 // TPB
-KICKS = (2, 1, 1, 1)
+XPIECES = {0: (0, 9), 1: (9, 18), 4: (18, 27), 5: (27, FR)}
 
 
 def tile_gccgc_pa_kernel(tc, x_pad, rel, A, w3, b3, out):
@@ -36,14 +36,14 @@ def tile_gccgc_pa_kernel(tc, x_pad, rel, A, w3, b3, out):
         const = ctx.enter_context(tc.tile_pool(name="const", bufs=1))
         rpool = ctx.enter_context(tc.tile_pool(name="rpool", bufs=3))
         work = ctx.enter_context(tc.tile_pool(name="work", bufs=2))
-        ypool = ctx.enter_context(tc.tile_pool(name="ypool", bufs=4))
+        qpool = ctx.enter_context(tc.tile_pool(name="qpool", bufs=3))
+        ypool = ctx.enter_context(tc.tile_pool(name="ypool", bufs=8))
         psw = ctx.enter_context(tc.psum_pool(name="psw", bufs=3))
-        psx = ctx.enter_context(tc.psum_pool(name="psx", bufs=2))
+        psx = ctx.enter_context(tc.psum_pool(name="psx", bufs=3))
         psz = ctx.enter_context(tc.psum_pool(name="psz", bufs=2))
-        psj = ctx.enter_context(tc.psum_pool(name="psj", bufs=1))
 
         r_t, pn_t, xt_t, xp_t = {}, {}, {}, {}
-        inw_t, inx_t, q_t = {}, {}, {}
+        inw_t, inx_t, xq_t, wq_t = {}, {}, {}, {}
 
         def load_rel(n):
             r = rpool.tile([P, 4096], BF16, name="r")
@@ -51,23 +51,23 @@ def tile_gccgc_pa_kernel(tc, x_pad, rel, A, w3, b3, out):
             r_t[n] = r
 
         def load_x(k, lo, hi):
-            if lo == 0:
-                xt_t[k] = work.tile([P, XG * XE], BF16, name="xt")
-                xp_t[k] = work.tile([P, XG * XE], BF16, name="xp")
-            xtv = xt_t[k][:].rearrange("p (n e) -> p n e", n=XG)
+            xt = work.tile([P, XG * XE], BF16, name="xt")
+            xtv = xt[:].rearrange("p (n e) -> p n e", n=XG)
             for tt in range(4):
                 nc.sync.dma_start(
                     out=xtv[tt:P:4, lo:hi, :], in_=xv[:, XG * k + lo : XG * k + hi, 128 * tt : 128 * tt + XE]
                 )
+            for g in range(lo, hi):
+                xt_t[XG * k + g] = xt
 
-        def perm_x(n, eng):
-            k, e0 = n // XG, (n % XG) * XE
-            dst = xp_t[k][:, e0 : e0 + XE].rearrange("p (f m e a) -> p f m a e", m=2, e=4, a=4)
-            src = xt_t[k][:, e0 : e0 + XE].rearrange("p (f a m e) -> p f m a e", m=2, e=4, a=4)
-            if eng == "v":
-                nc.vector.tensor_copy(out=dst, in_=src)
-            else:
-                nc.scalar.copy(out=dst, in_=src)
+        def perm_x(n, lo, hi):
+            e0 = (n % XG) * XE
+            if lo == 0:
+                xp_t[n] = work.tile([P, XE], BF16, name="xp")
+            nc.scalar.copy(
+                out=xp_t[n][:].rearrange("p (f m e a) -> p f m a e", m=2, e=4, a=4)[:, lo:hi],
+                in_=xt_t[n][:, e0 : e0 + XE].rearrange("p (f a m e) -> p f m a e", m=2, e=4, a=4)[:, lo:hi],
+            )
 
         def perm_w(n, b, eng):
             if b == 0:
@@ -81,13 +81,15 @@ def tile_gccgc_pa_kernel(tc, x_pad, rel, A, w3, b3, out):
 
         az = const.tile([P, P], BF16, name="az")
         nc.vector.memset(az[:], 0.0)
+        warm = const.tile([P, 1], BF16, name="warm")
+        nc.scalar.copy(out=warm[:], in_=az[:, P - 1 : P])
         bz = const.tile([P, P], BF16, name="bz")
         nc.vector.memset(bz[:], 0.0)
-        nc.sync.dma_start(out=az[0:32, 0:32], in_=A)
         load_x(0, 0, 1)
+        nc.sync.dma_start(out=az[0:32, 0:32], in_=A)
         load_rel(0)
-        load_x(0, 1, XG)
         load_rel(1)
+        load_x(0, 1, XG)
         load_x(1, 0, XG)
         nc.sync.dma_start(out=bz[0:8, :], in_=b3v)
 
@@ -96,19 +98,17 @@ def tile_gccgc_pa_kernel(tc, x_pad, rel, A, w3, b3, out):
         onec = const.tile([P, 512], U32, name="onec", align_bytes=64)
         ones_s = const.tile([P, 512], U8, name="ones_s", align_bytes=64)
         nc.vector.quantize_mx(out=onec[:].bitcast(FP8X4), scales=ones_s[:], in_=ones[:])
-        junk = psj.tile([P, 512], F32, name="junk")
 
-        def kick(times):
-            for rep in range(times):
-                nc.tensor.matmul_mx(
-                    out=junk[:],
-                    lhsT=onec[:, 0:P].bitcast(FP8X4),
-                    lhsT_scale=ones_s[:, 0:P],
-                    rhs=onec[:].bitcast(FP8X4),
-                    rhs_scale=ones_s[:],
-                    start=True,
-                    stop=True,
-                )
+        def kick(out):
+            nc.tensor.matmul_mx(
+                out=out,
+                lhsT=onec[:, 0:P].bitcast(FP8X4),
+                lhsT_scale=ones_s[:, 0:P],
+                rhs=onec[:, 0 : out.shape[1]].bitcast(FP8X4),
+                rhs_scale=ones_s[:, 0 : out.shape[1]],
+                start=True,
+                stop=True,
+            )
 
         ident_b = const.tile([P, P], BF16, name="ident_b")
         make_identity(nc, ident_b[:])
@@ -132,11 +132,9 @@ def tile_gccgc_pa_kernel(tc, x_pad, rel, A, w3, b3, out):
         acol = const.tile([P, 32], F32, name="acol")
         nc.vector.tensor_copy(out=acol[:], in_=ps2[:, 0:32])
 
-        perm_x(0, "v")
+        perm_x(0, 0, FR)
         for b in range(NB):
-            perm_w(0, b, "v")
-        for n in range(1, XG):
-            perm_x(n, "s")
+            perm_w(0, b, "s" if b % 4 == 3 else "v")
 
         zc = const.tile([P, 4096], BF16, name="zc")
         zcv = zc[:].rearrange("p (i g) -> p i g", g=P)
@@ -166,11 +164,17 @@ def tile_gccgc_pa_kernel(tc, x_pad, rel, A, w3, b3, out):
         zp_t = {}
 
         def first_products(n, q):
-            xc, xs, wc, ws = q_t[n]
             hb = q // 2
             if q % 2 == 0:
                 zp_t[hb] = psz.tile([P, 512], F32, name="zp")
+            if n < NG - 2:
+                for rep in range(2 if q != 2 else 1):
+                    kick(zp_t[hb][:] if q % 2 == 0 else zp_t[hb][:, 256:512])
+            if n < 0:
+                return
             zp = zp_t[hb]
+            xc, xs = xq_t[n]
+            wc, ws = wq_t[n]
             for s in (2 * (q % 2), 2 * (q % 2) + 1):
                 cols = slice((4 * hb + s) * P, (4 * hb + s + 1) * P)
                 nc.tensor.matmul_mx(
@@ -183,120 +187,159 @@ def tile_gccgc_pa_kernel(tc, x_pad, rel, A, w3, b3, out):
                     stop=True,
                 )
             if q % 2 == 1:
+                zpv = zp[:].rearrange("p (g c i) -> p c i g", g=4, c=4, i=32)
+                if n == NG - 1:
+                    g0 = 8 * n + 4 * hb
+                    for c4 in range(4):
+                        rows = slice(32 * c4, 32 * c4 + 32)
+                        if hb == 0:
+                            nc.scalar.copy(out=zcv[rows, :, g0 : g0 + 4], in_=zpv[rows, c4, :, :])
+                        else:
+                            nc.vector.tensor_copy(out=zcv[rows, :, g0 : g0 + 4], in_=zpv[rows, c4, :, :])
+                    return
                 if n % 4 == 0 and hb == 0:
                     zs_t[n // 4] = work.tile([P, 4096], BF16, name="zs")
                 zsv = zs_t[n // 4][:].rearrange("p (c i g) -> p c i g", c=4, i=32, g=32)
                 g0 = 8 * (n % 4) + 4 * hb
                 for c4 in range(4):
-                    nc.scalar.copy(
-                        out=zsv[:, c4, :, g0 : g0 + 4],
-                        in_=zp[:].rearrange("p (g c i) -> p c i g", g=4, c=4, i=32)[:, c4, :, :],
-                    )
+                    nc.scalar.copy(out=zsv[:, c4, :, g0 : g0 + 4], in_=zpv[:, c4, :, :])
 
-        def merge_z(k):
-            zsv = zs_t[k][:].rearrange("p (c i g) -> p c i g", c=4, i=32, g=32)
+        def merge_z(n, groups):
+            zsv = zs_t[n // 4][:].rearrange("p (c i g) -> p c i g", c=4, i=32, g=32)
+            g0 = 8 * (n % 4)
             for c4 in (1, 2, 3, 0):
                 rows = slice(32 * c4, 32 * c4 + 32)
-                nc.vector.tensor_copy(out=zcv[rows, :, 32 * k : 32 * (k + 1)], in_=zsv[rows, c4, :, :])
+                nc.vector.tensor_copy(
+                    out=zcv[rows, :, 8 * n : 8 * (n + groups)], in_=zsv[rows, c4, :, g0 : g0 + 8 * groups]
+                )
 
-        def quantise(n, piece):
-            if piece == 0:
-                q_t[n] = (
-                    work.tile([P, 1024], U32, name="xc", align_bytes=64),
-                    work.tile([P, 1024], U8, name="xs", align_bytes=64),
+        def quantise_x(n, h):
+            if h == 0:
+                xq_t[n] = (
+                    qpool.tile([P, 1024], U32, name="xc", align_bytes=64),
+                    qpool.tile([P, 1024], U8, name="xs", align_bytes=64),
+                )
+            xc, xs = xq_t[n]
+            nc.vector.quantize_mx(
+                out=xc[:, 512 * h : 512 * (h + 1)].bitcast(FP8X4),
+                scales=xs[:, 512 * h : 512 * (h + 1)],
+                in_=inx_t[n][:, 2048 * h : 2048 * (h + 1)],
+            )
+
+        def quantise_w(n, h):
+            if h == 0:
+                wq_t[n] = (
                     work.tile([P, 1024], U32, name="wc", align_bytes=64),
                     work.tile([P, 1024], U8, name="ws", align_bytes=64),
                 )
-            xc, xs, wc, ws = q_t[n]
-            h = piece // 2
-            codes, scales, values = (xc, xs, inx_t[n]) if piece % 2 == 0 else (wc, ws, inw_t[n])
+            wc, ws = wq_t[n]
             nc.vector.quantize_mx(
-                out=codes[:, 512 * h : 512 * (h + 1)].bitcast(FP8X4),
-                scales=scales[:, 512 * h : 512 * (h + 1)],
-                in_=values[:, 2048 * h : 2048 * (h + 1)],
+                out=wc[:, 512 * h : 512 * (h + 1)].bitcast(FP8X4),
+                scales=ws[:, 512 * h : 512 * (h + 1)],
+                in_=inw_t[n][:, 2048 * h : 2048 * (h + 1)],
             )
 
-        for n in range(NG + 1):
+        def windows_x(n, b, eng):
+            if b == 0:
+                inx_t[n] = work.tile([P, 4096], BF16, name="inx", align_bytes=64)
+            xp = xp_t[n]
+            xtp = psx.tile([P, TPB * P], BF16, name="xtp")
+            for s in range(TPB):
+                t = TPB * b + s
+                nc.tensor.transpose(xtp[:, s * P : (s + 1) * P], xp[:, 32 * t : 32 * t + P], ident_b[:])
+            inxw = inx_t[n][:].bitcast(F32).rearrange("p (c t u) -> p c t u", c=32, t=32, u=2)
+            dst = inxw[:, :, TPB * b : TPB * (b + 1), :]
+            src = xtp[:].bitcast(F32).rearrange("p (s c u) -> p c s u", s=TPB, c=32, u=2)
+            if eng == "v":
+                nc.vector.tensor_copy(out=dst, in_=src)
+            else:
+                nc.scalar.copy(out=dst, in_=src)
+
+        for n in range(NG):
             if n + 2 < NG:
                 load_rel(n + 2)
             if n % XG == XG - 1 and n // XG + 2 < NG // XG:
                 load_x(n // XG + 2, 0, XG)
             if n == 1:
                 nc.sync.dma_start(out=w3r[:].rearrange("p (t c) -> p t c", t=8), in_=w3v)
-            if n < NG:
-                pv = pn_t[n][:].rearrange("p (i k) -> p i k", i=32)
-                xp = xp_t[n // XG]
-                x0 = (n % XG) * XE
-                inw_t[n] = work.tile([P, 4096], BF16, name="inw", align_bytes=64)
-                inwv = inw_t[n][:].rearrange("p (c i t) -> p c i t", c=32, i=32, t=4)
-                inx_t[n] = work.tile([P, 4096], BF16, name="inx", align_bytes=64)
-                inxw = inx_t[n][:].bitcast(F32).rearrange("p (c t u) -> p c t u", c=32, t=32, u=2)
+            pv = pn_t[n][:].rearrange("p (i k) -> p i k", i=32)
+            inw_t[n] = work.tile([P, 4096], BF16, name="inw", align_bytes=64)
+            inwv = inw_t[n][:].rearrange("p (c i t) -> p c i t", c=32, i=32, t=4)
             for b in range(NB):
-                if n < NG:
-                    wtp = psw.tile([P, TPB * P], BF16, name="wtp")
-                    for s in range(TPB):
-                        i = TPB * b + s
-                        nc.tensor.transpose(wtp[:, s * P : (s + 1) * P], pv[:, i, :], ident_b[:])
-                    xtp = psx.tile([P, TPB * P], BF16, name="xtp")
-                    for s in range(TPB):
-                        t = TPB * b + s
-                        nc.tensor.transpose(
-                            xtp[:, s * P : (s + 1) * P], xp[:, x0 + 32 * t : x0 + 32 * t + P], ident_b[:]
-                        )
-                    nc.vector.tensor_tensor(
-                        out=inwv[:, :, TPB * b : TPB * (b + 1), :],
-                        in0=wtp[:].rearrange("p (s c t) -> p c s t", s=TPB, c=32, t=4),
-                        in1=arep[:, 4 * TPB * b : 4 * TPB * (b + 1)]
-                        .rearrange("p (s t) -> p s t", t=4)
-                        .unsqueeze(1)
-                        .to_broadcast([P, 32, TPB, 4]),
-                        op=ADD,
-                    )
-                    nc.scalar.copy(
-                        out=inxw[:, :, TPB * b : TPB * (b + 1), :],
-                        in_=xtp[:].bitcast(F32).rearrange("p (s c u) -> p c s u", s=TPB, c=32, u=2),
-                    )
-                if 1 <= n <= NG and b % 2 == 0:
-                    quantise(n - 1, b // 2)
+                if n == 0:
+                    windows_x(0, b, "sv"[b % 2])
+                    if b == 3:
+                        perm_x(1, 0, FR)
+                wtp = psw.tile([P, TPB * P], BF16, name="wtp")
+                for s in range(TPB):
+                    i = TPB * b + s
+                    nc.tensor.transpose(wtp[:, s * P : (s + 1) * P], pv[:, i, :], ident_b[:])
+                nc.vector.tensor_tensor(
+                    out=inwv[:, :, TPB * b : TPB * (b + 1), :],
+                    in0=wtp[:].rearrange("p (s c t) -> p c s t", s=TPB, c=32, t=4),
+                    in1=arep[:, 4 * TPB * b : 4 * TPB * (b + 1)]
+                    .rearrange("p (s t) -> p s t", t=4)
+                    .unsqueeze(1)
+                    .to_broadcast([P, 32, TPB, 4]),
+                    op=ADD,
+                )
+                if n == 0 and b >= 4:
+                    windows_x(1, 2 * (b - 4), "s")
+                    windows_x(1, 2 * (b - 4) + 1, "v")
+                if 1 <= n < NG - 1:
+                    windows_x(n + 1, b, "s")
+                if n >= 1 and b % 4 == 0:
+                    quantise_x(n, b // 4)
+                if n >= 1 and b % 4 == 2:
+                    quantise_w(n - 1, b // 4)
                 if n + 1 < NG:
                     perm_w(n + 1, b, "s" if b in (2, 6) else "v")
                 if b % 2 == 1:
-                    if 2 <= n:
-                        first_products(n - 2, b // 2)
-                    if n < NG:
-                        kick(KICKS[b // 2])
-                if b == 2 and n >= 6 and n % 4 == 2:
-                    merge_z((n - 6) // 4)
-                if b == 4 and n + XG < NG:
-                    perm_x(n + XG, "s")
+                    first_products(n - 2, b // 2)
+                if b == 3 and n >= 6 and n % 4 == 2:
+                    merge_z(n - 6, 4)
+                if n == 0 and b == 7:
+                    perm_x(2, 0, FR)
+                if n >= 1 and n + 2 < NG and b in XPIECES:
+                    perm_x(n + 2, *XPIECES[b])
                 if b == 6:
                     if n == 2:
                         prepare_b3()
                     if 3 <= n < 7:
                         prepare_w3(n - 3)
+            if n == 0:
+                quantise_x(0, 0)
+                quantise_x(0, 1)
             if n == 7:
                 nc.vector.quantize_mx(out=w3c[:].bitcast(FP8X4), scales=w3s[:], in_=inw3[:])
 
+        quantise_w(NG - 1, 0)
+        quantise_w(NG - 1, 1)
+        for q in range(4):
+            first_products(NG - 2, q)
         for q in range(4):
             first_products(NG - 1, q)
-        merge_z(3)
-        banks = [(psw, "wtp"), (psx, "xtp"), (psz, "zp"), (psw, "wtp"), (psx, "xtp"), (psz, "zp"), (psw, "wtp"), (psj, "junk")]
+            if q == 0:
+                merge_z(NG - 4, 3)
+
+        junk = psx.tile([P, 512], F32, name="junk", tag="xtp")
+        for rep in range(3):
+            kick(junk[:])
         inz = const.tile([P, 4096], BF16, name="inz", align_bytes=64)
         inzv = inz[:].rearrange("p (t i c) -> p t i c", t=32, i=32, c=4)
         zts = []
-        for b in range(8):
-            pool, tag = banks[b]
-            zt = pool.tile([P, 512], BF16, name="zt", tag=tag)
-            for s in range(4):
-                i = 4 * b + s
-                nc.tensor.transpose(zt[:, s * P : (s + 1) * P], zc[:, i * P : (i + 1) * P], ident_b[:])
+        for b in range(4):
+            pool, tag = ((psw, "wtp"), (psx, "xtp"))[b % 2]
+            zt = pool.tile([P, 1024], BF16, name="zt", tag=tag)
+            for s in range(8):
+                nc.tensor.transpose(zt[:, s * P : (s + 1) * P], zcv[:, 8 * b + s, :], ident_b[:])
             zts.append(zt)
         zq = const.tile([P, 1024], U32, name="zq", align_bytes=64)
         zs = const.tile([P, 1024], U8, name="zs", align_bytes=64)
         for h in range(2):
-            for b in range(8):
-                src = zts[b][:].rearrange("p (s c t) -> p t s c", s=4, c=4, t=32)[:, 16 * h : 16 * h + 16, :, :]
-                dst = inzv[:, 16 * h : 16 * h + 16, 4 * b : 4 * b + 4, :]
+            for b in range(4):
+                src = zts[b][:].rearrange("p (s c t) -> p t s c", s=8, c=4, t=32)[:, 16 * h : 16 * h + 16, :, :]
+                dst = inzv[:, 16 * h : 16 * h + 16, 8 * b : 8 * b + 8, :]
                 if b % 2 == 0:
                     nc.vector.tensor_copy(out=dst, in_=src)
                 else:
@@ -306,6 +349,7 @@ def tile_gccgc_pa_kernel(tc, x_pad, rel, A, w3, b3, out):
                 scales=zs[:, 512 * h : 512 * (h + 1)],
                 in_=inz[:, 2048 * h : 2048 * (h + 1)],
             )
+        banks = [(psz, "zp"), (psw, "wtp"), (psx, "xtp"), (psz, "zp"), (psw, "wtp"), (psx, "xtp"), (psw, "wtp"), (psx, "xtp")]
         k = 0
         for h in range(2):
             for ot in range(8):

@@ -137,7 +137,8 @@ def tile_gccgc_pa_kernel(tc, x_pad, rel, A, w3, b3, out):
             perm_w(0, b, "s" if b % 4 == 3 else "v")
 
         zc = const.tile([P, 4096], BF16, name="zc")
-        zcv = zc[:].rearrange("p (i g) -> p i g", g=P)
+        zcv = zc[:].rearrange("p (g i) -> p g i", g=P)
+        zcw = zc[:].bitcast(F32).rearrange("p (g w) -> p g w", g=P)
         zs_t = {}
         b3f = const.tile([P, 8], F32, name="b3f")
         w3c = const.tile([P, 1024], U32, name="w3c", align_bytes=64)
@@ -161,21 +162,16 @@ def tile_gccgc_pa_kernel(tc, x_pad, rel, A, w3, b3, out):
                 in_=w3p[:].rearrange("p (t u o) -> p t o u", t=2, u=2, o=P),
             )
 
-        zp_t = {}
-
-        def first_products(n, q):
-            hb = q // 2
-            if q % 2 == 0:
-                zp_t[hb] = psz.tile([P, 512], F32, name="zp")
+        def first_products(n, hb):
+            zp = psz.tile([P, 512], F32, name="zp")
             if n < NG - 2:
-                for rep in range(2 if q != 2 else 1):
-                    kick(zp_t[hb][:] if q % 2 == 0 else zp_t[hb][:, 256:512])
+                kick(zp[:])
+                kick(zp[:])
             if n < 0:
                 return
-            zp = zp_t[hb]
             xc, xs = xq_t[n]
             wc, ws = wq_t[n]
-            for s in (2 * (q % 2), 2 * (q % 2) + 1):
+            for s in range(4):
                 cols = slice((4 * hb + s) * P, (4 * hb + s + 1) * P)
                 nc.tensor.matmul_mx(
                     out=zp[:, s * P : (s + 1) * P],
@@ -186,31 +182,28 @@ def tile_gccgc_pa_kernel(tc, x_pad, rel, A, w3, b3, out):
                     start=True,
                     stop=True,
                 )
-            if q % 2 == 1:
-                zpv = zp[:].rearrange("p (g c i) -> p c i g", g=4, c=4, i=32)
-                if n == NG - 1:
-                    g0 = 8 * n + 4 * hb
-                    for c4 in range(4):
-                        rows = slice(32 * c4, 32 * c4 + 32)
-                        if hb == 0:
-                            nc.scalar.copy(out=zcv[rows, :, g0 : g0 + 4], in_=zpv[rows, c4, :, :])
-                        else:
-                            nc.vector.tensor_copy(out=zcv[rows, :, g0 : g0 + 4], in_=zpv[rows, c4, :, :])
-                    return
-                if n % 4 == 0 and hb == 0:
-                    zs_t[n // 4] = work.tile([P, 4096], BF16, name="zs")
-                zsv = zs_t[n // 4][:].rearrange("p (c i g) -> p c i g", c=4, i=32, g=32)
-                g0 = 8 * (n % 4) + 4 * hb
+            if n == NG - 1:
+                g0 = 8 * n + 4 * hb
+                zpv = zp[:].rearrange("p (g c i) -> p g c i", g=4, c=4, i=32)
                 for c4 in range(4):
-                    nc.scalar.copy(out=zsv[:, c4, :, g0 : g0 + 4], in_=zpv[:, c4, :, :])
+                    rows = slice(32 * c4, 32 * c4 + 32)
+                    if hb == 0:
+                        nc.scalar.copy(out=zcv[rows, g0 : g0 + 4, :], in_=zpv[rows, :, c4, :])
+                    else:
+                        nc.vector.tensor_copy(out=zcv[rows, g0 : g0 + 4, :], in_=zpv[rows, :, c4, :])
+                return
+            if n % 4 == 0 and hb == 0:
+                zs_t[n // 4] = work.tile([P, 4096], BF16, name="zs")
+            g0 = 8 * (n % 4) + 4 * hb
+            nc.scalar.copy(out=zs_t[n // 4][:, g0 * P : (g0 + 4) * P], in_=zp[:])
 
         def merge_z(n, groups):
-            zsv = zs_t[n // 4][:].rearrange("p (c i g) -> p c i g", c=4, i=32, g=32)
+            zsv = zs_t[n // 4][:].rearrange("p (g c i) -> p g c i", g=32, c=4)
             g0 = 8 * (n % 4)
             for c4 in (1, 2, 3, 0):
                 rows = slice(32 * c4, 32 * c4 + 32)
                 nc.vector.tensor_copy(
-                    out=zcv[rows, :, 8 * n : 8 * (n + groups)], in_=zsv[rows, c4, :, g0 : g0 + 8 * groups]
+                    out=zcv[rows, 8 * n : 8 * (n + groups), :], in_=zsv[rows, g0 : g0 + 8 * groups, c4, :]
                 )
 
         def quantise_x(n, h):
@@ -267,7 +260,7 @@ def tile_gccgc_pa_kernel(tc, x_pad, rel, A, w3, b3, out):
             inwv = inw_t[n][:].rearrange("p (c i t) -> p c i t", c=32, i=32, t=4)
             for b in range(NB):
                 if n == 0:
-                    windows_x(0, b, "sv"[b % 2])
+                    windows_x(0, b, "v" if b % 4 == 1 else "s")
                     if b == 3:
                         perm_x(1, 0, FR)
                 wtp = psw.tile([P, TPB * P], BF16, name="wtp")
@@ -285,7 +278,7 @@ def tile_gccgc_pa_kernel(tc, x_pad, rel, A, w3, b3, out):
                 )
                 if n == 0 and b >= 4:
                     windows_x(1, 2 * (b - 4), "s")
-                    windows_x(1, 2 * (b - 4) + 1, "v")
+                    windows_x(1, 2 * (b - 4) + 1, "v" if b % 2 == 1 else "s")
                 if 1 <= n < NG - 1:
                     windows_x(n + 1, b, "s")
                 if n >= 1 and b % 4 == 0:
@@ -294,8 +287,8 @@ def tile_gccgc_pa_kernel(tc, x_pad, rel, A, w3, b3, out):
                     quantise_w(n - 1, b // 4)
                 if n + 1 < NG:
                     perm_w(n + 1, b, "s" if b in (2, 6) else "v")
-                if b % 2 == 1:
-                    first_products(n - 2, b // 2)
+                if b % 4 == 3:
+                    first_products(n - 2, b // 4)
                 if b == 3 and n >= 6 and n % 4 == 2:
                     merge_z(n - 6, 4)
                 if n == 0 and b == 7:
@@ -315,12 +308,11 @@ def tile_gccgc_pa_kernel(tc, x_pad, rel, A, w3, b3, out):
 
         quantise_w(NG - 1, 0)
         quantise_w(NG - 1, 1)
-        for q in range(4):
-            first_products(NG - 2, q)
-        for q in range(4):
-            first_products(NG - 1, q)
-            if q == 0:
-                merge_z(NG - 4, 3)
+        for hb in range(2):
+            first_products(NG - 2, hb)
+        merge_z(NG - 4, 3)
+        for hb in range(2):
+            first_products(NG - 1, hb)
 
         junk = psx.tile([P, 512], F32, name="junk", tag="xtp")
         for rep in range(3):
@@ -330,16 +322,16 @@ def tile_gccgc_pa_kernel(tc, x_pad, rel, A, w3, b3, out):
         zts = []
         for b in range(4):
             pool, tag = ((psw, "wtp"), (psx, "xtp"))[b % 2]
-            zt = pool.tile([P, 1024], BF16, name="zt", tag=tag)
-            for s in range(8):
-                nc.tensor.transpose(zt[:, s * P : (s + 1) * P], zcv[:, 8 * b + s, :], ident_b[:])
+            zt = pool.tile([P, 512], F32, name="zt", tag=tag)
+            for s in range(4):
+                nc.tensor.transpose(zt[:, s * P : (s + 1) * P], zcw[:, :, 4 * b + s], ident_f[:])
             zts.append(zt)
         zq = const.tile([P, 1024], U32, name="zq", align_bytes=64)
         zs = const.tile([P, 1024], U8, name="zs", align_bytes=64)
         for h in range(2):
             for b in range(4):
-                src = zts[b][:].rearrange("p (s c t) -> p t s c", s=8, c=4, t=32)[:, 16 * h : 16 * h + 16, :, :]
-                dst = inzv[:, 16 * h : 16 * h + 16, 8 * b : 8 * b + 8, :]
+                src = zts[b][:].bitcast(BF16).rearrange("p (s c t u) -> p t s u c", s=4, c=4, t=32, u=2)[:, 16 * h : 16 * h + 16]
+                dst = inzv[:, 16 * h : 16 * h + 16, 8 * b : 8 * b + 8, :].rearrange("p t (s u) c -> p t s u c", u=2)
                 if b % 2 == 0:
                     nc.vector.tensor_copy(out=dst, in_=src)
                 else:

from contextlib import ExitStack

import concourse.mybir as mybir
from concourse.masks import make_identity

FLOPS = 2 * 512 * 32 * 512 * 32 + 2 * 1024 * 512 * 1024

BF16 = mybir.dt.bfloat16
F32 = mybir.dt.float32
U32 = mybir.dt.uint32
U8 = mybir.dt.uint8
FP8X4 = mybir.dt.float8_e4m3fn_x4
ADD = mybir.AluOpType.add
IDENTITY = mybir.ActivationFunctionType.Identity

P = 128
NG = 16
XG = 4
FR = 35
XE = FR * 32
TPB = 4
NB = 32 // TPB
XPIECES = {0: (0, 9), 1: (9, 18), 4: (18, 27), 5: (27, FR)}


def tile_gccgc_pa_kernel(tc, x_pad, rel, A, w3, b3, out):
    nc = tc.nc
    relv = rel.rearrange("b (n r q) j i -> r (b n) (q j i)", r=P, q=4)
    xv = x_pad.rearrange("b (n c) f j -> c (b n) (f j)", c=32)
    w3v = w3.rearrange("(t p) c -> p t c", p=P)
    b3v = b3.rearrange("(t p) -> t p", p=P)
    outv = out.rearrange("b (t p) f i -> p (b t) (f i)", p=P)

    with ExitStack() as ctx:
        ctx.enter_context(tc.manual_schedule())
        const = ctx.enter_context(tc.tile_pool(name="const", bufs=1))
        rpool = ctx.enter_context(tc.tile_pool(name="rpool", bufs=3))
        work = ctx.enter_context(tc.tile_pool(name="work", bufs=2))
        qpool = ctx.enter_context(tc.tile_pool(name="qpool", bufs=3))
        ypool = ctx.enter_context(tc.tile_pool(name="ypool", bufs=8))
        psw = ctx.enter_context(tc.psum_pool(name="psw", bufs=3))
        psx = ctx.enter_context(tc.psum_pool(name="psx", bufs=3))
        psz = ctx.enter_context(tc.psum_pool(name="psz", bufs=2))

        r_t, pn_t, xt_t, xp_t = {}, {}, {}, {}
        inw_t, inx_t, xq_t, wq_t = {}, {}, {}, {}

        def load_rel(n):
            r = rpool.tile([P, 4096], BF16, name="r")
            nc.sync.dma_start(out=r[:], in_=relv[:, n, :])
            r_t[n] = r

        def load_x(k, lo, hi):
            xt = work.tile([P, XG * XE], BF16, name="xt")
            xtv = xt[:].rearrange("p (n e) -> p n e", n=XG)
            for tt in range(4):
                nc.sync.dma_start(
                    out=xtv[tt:P:4, lo:hi, :], in_=xv[:, XG * k + lo : XG * k + hi, 128 * tt : 128 * tt + XE]
                )
            for g in range(lo, hi):
                xt_t[XG * k + g] = xt

        def perm_x(n, lo, hi):
            e0 = (n % XG) * XE
            if lo == 0:
                xp_t[n] = work.tile([P, XE], BF16, name="xp")
            nc.scalar.copy(
                out=xp_t[n][:].rearrange("p (f m e a) -> p f m a e", m=2, e=4, a=4)[:, lo:hi],
                in_=xt_t[n][:, e0 : e0 + XE].rearrange("p (f a m e) -> p f m a e", m=2, e=4, a=4)[:, lo:hi],
            )

        def perm_w(n, b, eng):
            if b == 0:
                pn_t[n] = work.tile([P, 4096], BF16, name="pn")
            dst = pn_t[n][:].rearrange("p (i v q m a) -> p i q m a v", i=8, v=4, q=4, m=8, a=4)[:, b]
            src = r_t[n][:].rearrange("p (q a m i v) -> p i q m a v", q=4, a=4, m=8, i=8, v=4)[:, b]
            if eng == "v":
                nc.vector.tensor_copy(out=dst, in_=src)
            else:
                nc.scalar.copy(out=dst, in_=src)

        az = const.tile([P, P], BF16, name="az")
        nc.vector.memset(az[:], 0.0)
        warm = const.tile([P, 1], BF16, name="warm")
        nc.scalar.copy(out=warm[:], in_=az[:, P - 1 : P])
        bz = const.tile([P, P], BF16, name="bz")
        nc.vector.memset(bz[:], 0.0)
        load_x(0, 0, 1)
        nc.sync.dma_start(out=az[0:32, 0:32], in_=A)
        load_rel(0)
        load_rel(1)
        load_x(0, 1, XG)
        load_x(1, 0, XG)
        nc.sync.dma_start(out=bz[0:8, :], in_=b3v)

        ones = const.tile([P, 2048], BF16, name="ones", align_bytes=64)
        nc.vector.memset(ones[:], 1.0)
        onec = const.tile([P, 512], U32, name="onec", align_bytes=64)
        ones_s = const.tile([P, 512], U8, name="ones_s", align_bytes=64)
        nc.vector.quantize_mx(out=onec[:].bitcast(FP8X4), scales=ones_s[:], in_=ones[:])

        def kick(out):
            nc.tensor.matmul_mx(
                out=out,
                lhsT=onec[:, 0:P].bitcast(FP8X4),
                lhsT_scale=ones_s[:, 0:P],
                rhs=onec[:, 0 : out.shape[1]].bitcast(FP8X4),
                rhs_scale=ones_s[:, 0 : out.shape[1]],
                start=True,
                stop=True,
            )

        ident_b = const.tile([P, P], BF16, name="ident_b")
        make_identity(nc, ident_b[:])
        ident_f = const.tile([P, P], F32, name="ident_f")
        make_identity(nc, ident_f[:])

        ps1 = psz.tile([P, P], BF16, name="ps1", tag="zp")
        nc.tensor.transpose(ps1[:], az[:], ident_b[:])
        atr = const.tile([P, P], BF16, name="atr")
        nc.vector.tensor_copy(
            out=atr[:].rearrange("p (q m a) -> p q m a", q=4, m=8, a=4),
            in_=ps1[:, 0:32].rearrange("p (a m) -> p m a", a=4).unsqueeze(1).to_broadcast([P, 4, 8, 4]),
        )
        ps2 = psz.tile([P, P], BF16, name="ps2", tag="zp")
        nc.tensor.transpose(ps2[:], atr[:], ident_b[:])
        arep = const.tile([P, P], BF16, name="arep")
        nc.vector.tensor_copy(
            out=arep[:].rearrange("p (i t) -> p i t", t=4),
            in_=ps2[:, 0:32].unsqueeze(2).to_broadcast([P, 32, 4]),
        )
        acol = const.tile([P, 32], F32, name="acol")
        nc.vector.tensor_copy(out=acol[:], in_=ps2[:, 0:32])

        perm_x(0, 0, FR)
        for b in range(NB):
            perm_w(0, b, "s" if b % 4 == 3 else "v")

        zc = const.tile([P, 4096], BF16, name="zc")
        zcv = zc[:].rearrange("p (g i) -> p g i", g=P)
        zcw = zc[:].bitcast(F32).rearrange("p (g w) -> p g w", g=P)
        zs_t = {}
        b3f = const.tile([P, 8], F32, name="b3f")
        w3c = const.tile([P, 1024], U32, name="w3c", align_bytes=64)
        w3s = const.tile([P, 1024], U8, name="w3s", align_bytes=64)
        w3r = const.tile([P, 4096], BF16, name="w3r")
        w3w = w3r[:].bitcast(F32).rearrange("p (t q u) -> p t q u", t=8, q=P, u=2)
        inw3 = const.tile([P, 4096], BF16, name="inw3", align_bytes=64)
        inw3w = inw3[:].bitcast(F32).rearrange("p (t o u) -> p t o u", t=8, o=P, u=2)

        def prepare_b3():
            ps3 = psz.tile([P, P], BF16, name="ps3", tag="zp")
            nc.tensor.transpose(ps3[:], bz[:], ident_b[:])
            nc.scalar.copy(out=b3f[:], in_=ps3[:, 0:8])

        def prepare_w3(tp):
            w3p = psz.tile([P, 512], F32, name="w3p", tag="zp")
            for s in range(4):
                nc.tensor.transpose(w3p[:, s * P : (s + 1) * P], w3w[:, 2 * tp + s // 2, :, s % 2], ident_f[:])
            nc.scalar.copy(
                out=inw3w[:, 2 * tp : 2 * tp + 2, :, :],
                in_=w3p[:].rearrange("p (t u o) -> p t o u", t=2, u=2, o=P),
            )

        def first_products(n, hb):
            zp = psz.tile([P, 512], F32, name="zp")
            if n < NG - 2:
                kick(zp[:])
                kick(zp[:])
            if n < 0:
                return
            xc, xs = xq_t[n]
            wc, ws = wq_t[n]
            for s in range(4):
                cols = slice((4 * hb + s) * P, (4 * hb + s + 1) * P)
                nc.tensor.matmul_mx(
                    out=zp[:, s * P : (s + 1) * P],
                    lhsT=xc[:, cols].bitcast(FP8X4),
                    lhsT_scale=xs[:, cols],
                    rhs=wc[:, cols].bitcast(FP8X4),
                    rhs_scale=ws[:, cols],
                    start=True,
                    stop=True,
                )
            if n == NG - 1:
                g0 = 8 * n + 4 * hb
                zpv = zp[:].rearrange("p (g c i) -> p g c i", g=4, c=4, i=32)
                for c4 in range(4):
                    rows = slice(32 * c4, 32 * c4 + 32)
                    if hb == 0:
                        nc.scalar.copy(out=zcv[rows, g0 : g0 + 4, :], in_=zpv[rows, :, c4, :])
                    else:
                        nc.vector.tensor_copy(out=zcv[rows, g0 : g0 + 4, :], in_=zpv[rows, :, c4, :])
                return
            if n % 4 == 0 and hb == 0:
                zs_t[n // 4] = work.tile([P, 4096], BF16, name="zs")
            g0 = 8 * (n % 4) + 4 * hb
            nc.scalar.copy(out=zs_t[n // 4][:, g0 * P : (g0 + 4) * P], in_=zp[:])

        def merge_z(n, groups):
            zsv = zs_t[n // 4][:].rearrange("p (g c i) -> p g c i", g=32, c=4)
            g0 = 8 * (n % 4)
            for c4 in (1, 2, 3, 0):
                rows = slice(32 * c4, 32 * c4 + 32)
                nc.vector.tensor_copy(
                    out=zcv[rows, 8 * n : 8 * (n + groups), :], in_=zsv[rows, g0 : g0 + 8 * groups, c4, :]
                )

        def quantise_x(n, h):
            if h == 0:
                xq_t[n] = (
                    qpool.tile([P, 1024], U32, name="xc", align_bytes=64),
                    qpool.tile([P, 1024], U8, name="xs", align_bytes=64),
                )
            xc, xs = xq_t[n]
            nc.vector.quantize_mx(
                out=xc[:, 512 * h : 512 * (h + 1)].bitcast(FP8X4),
                scales=xs[:, 512 * h : 512 * (h + 1)],
                in_=inx_t[n][:, 2048 * h : 2048 * (h + 1)],
            )

        def quantise_w(n, h):
            if h == 0:
                wq_t[n] = (
                    work.tile([P, 1024], U32, name="wc", align_bytes=64),
                    work.tile([P, 1024], U8, name="ws", align_bytes=64),
                )
            wc, ws = wq_t[n]
            nc.vector.quantize_mx(
                out=wc[:, 512 * h : 512 * (h + 1)].bitcast(FP8X4),
                scales=ws[:, 512 * h : 512 * (h + 1)],
                in_=inw_t[n][:, 2048 * h : 2048 * (h + 1)],
            )

        def windows_x(n, b, eng):
            if b == 0:
                inx_t[n] = work.tile([P, 4096], BF16, name="inx", align_bytes=64)
            xp = xp_t[n]
            xtp = psx.tile([P, TPB * P], BF16, name="xtp")
            for s in range(TPB):
                t = TPB * b + s
                nc.tensor.transpose(xtp[:, s * P : (s + 1) * P], xp[:, 32 * t : 32 * t + P], ident_b[:])
            inxw = inx_t[n][:].bitcast(F32).rearrange("p (c t u) -> p c t u", c=32, t=32, u=2)
            dst = inxw[:, :, TPB * b : TPB * (b + 1), :]
            src = xtp[:].bitcast(F32).rearrange("p (s c u) -> p c s u", s=TPB, c=32, u=2)
            if eng == "v":
                nc.vector.tensor_copy(out=dst, in_=src)
            else:
                nc.scalar.copy(out=dst, in_=src)

        for n in range(NG):
            if n + 2 < NG:
                load_rel(n + 2)
            if n % XG == XG - 1 and n // XG + 2 < NG // XG:
                load_x(n // XG + 2, 0, XG)
            if n == 1:
                nc.sync.dma_start(out=w3r[:].rearrange("p (t c) -> p t c", t=8), in_=w3v)
            pv = pn_t[n][:].rearrange("p (i k) -> p i k", i=32)
            inw_t[n] = work.tile([P, 4096], BF16, name="inw", align_bytes=64)
            inwv = inw_t[n][:].rearrange("p (c i t) -> p c i t", c=32, i=32, t=4)
            for b in range(NB):
                if n == 0:
                    windows_x(0, b, "v" if b % 4 == 1 else "s")
                    if b == 3:
                        perm_x(1, 0, FR)
                wtp = psw.tile([P, TPB * P], BF16, name="wtp")
                for s in range(TPB):
                    i = TPB * b + s
                    nc.tensor.transpose(wtp[:, s * P : (s + 1) * P], pv[:, i, :], ident_b[:])
                nc.vector.tensor_tensor(
                    out=inwv[:, :, TPB * b : TPB * (b + 1), :],
                    in0=wtp[:].rearrange("p (s c t) -> p c s t", s=TPB, c=32, t=4),
                    in1=arep[:, 4 * TPB * b : 4 * TPB * (b + 1)]
                    .rearrange("p (s t) -> p s t", t=4)
                    .unsqueeze(1)
                    .to_broadcast([P, 32, TPB, 4]),
                    op=ADD,
                )
                if n == 0 and b >= 4:
                    windows_x(1, 2 * (b - 4), "s")
                    windows_x(1, 2 * (b - 4) + 1, "v" if b % 2 == 1 else "s")
                if 1 <= n < NG - 1:
                    windows_x(n + 1, b, "s")
                if n >= 1 and b % 4 == 0:
                    quantise_x(n, b // 4)
                if n >= 1 and b % 4 == 2:
                    quantise_w(n - 1, b // 4)
                if n + 1 < NG:
                    perm_w(n + 1, b, "s" if b in (2, 6) else "v")
                if b % 4 == 3:
                    first_products(n - 2, b // 4)
                if b == 3 and n >= 6 and n % 4 == 2:
                    merge_z(n - 6, 4)
                if n == 0 and b == 7:
                    perm_x(2, 0, FR)
                if n >= 1 and n + 2 < NG and b in XPIECES:
                    perm_x(n + 2, *XPIECES[b])
                if b == 6:
                    if n == 2:
                        prepare_b3()
                    if 3 <= n < 7:
                        prepare_w3(n - 3)
            if n == 0:
                quantise_x(0, 0)
                quantise_x(0, 1)
            if n == 7:
                nc.vector.quantize_mx(out=w3c[:].bitcast(FP8X4), scales=w3s[:], in_=inw3[:])

        quantise_w(NG - 1, 0)
        quantise_w(NG - 1, 1)
        for hb in range(2):
            first_products(NG - 2, hb)
        merge_z(NG - 4, 3)
        for hb in range(2):
            first_products(NG - 1, hb)

        junk = psx.tile([P, 512], F32, name="junk", tag="xtp")
        for rep in range(3):
            kick(junk[:])
        inz = const.tile([P, 4096], BF16, name="inz", align_bytes=64)
        inzv = inz[:].rearrange("p (t i c) -> p t i c", t=32, i=32, c=4)
        zts = []
        for b in range(4):
            pool, tag = ((psw, "wtp"), (psx, "xtp"))[b % 2]
            zt = pool.tile([P, 512], F32, name="zt", tag=tag)
            for s in range(4):
                nc.tensor.transpose(zt[:, s * P : (s + 1) * P], zcw[:, :, 4 * b + s], ident_f[:])
            zts.append(zt)
        zq = const.tile([P, 1024], U32, name="zq", align_bytes=64)
        zs = const.tile([P, 1024], U8, name="zs", align_bytes=64)
        for h in range(2):
            for b in range(4):
                src = zts[b][:].bitcast(BF16).rearrange("p (s c t u) -> p t s u c", s=4, c=4, t=32, u=2)[:, 16 * h : 16 * h + 16]
                dst = inzv[:, 16 * h : 16 * h + 16, 8 * b : 8 * b + 8, :].rearrange("p t (s u) c -> p t s u c", u=2)
                if b % 2 == 0:
                    nc.vector.tensor_copy(out=dst, in_=src)
                else:
                    nc.scalar.copy(out=dst, in_=src)
            nc.vector.quantize_mx(
                out=zq[:, 512 * h : 512 * (h + 1)].bitcast(FP8X4),
                scales=zs[:, 512 * h : 512 * (h + 1)],
                in_=inz[:, 2048 * h : 2048 * (h + 1)],
            )
        banks = [(psz, "zp"), (psw, "wtp"), (psx, "xtp"), (psz, "zp"), (psw, "wtp"), (psx, "xtp"), (psw, "wtp"), (psx, "xtp")]
        k = 0
        for h in range(2):
            for ot in range(8):
                pool, tag = banks[k % 8]
                yp = pool.tile([P, 512], F32, name="yp", tag=tag)
                nc.tensor.matmul_mx(
                    out=yp[:],
                    lhsT=w3c[:, ot * P : (ot + 1) * P].bitcast(FP8X4),
                    lhsT_scale=w3s[:, ot * P : (ot + 1) * P],
                    rhs=zq[:, h * 512 : (h + 1) * 512].bitcast(FP8X4),
                    rhs_scale=zs[:, h * 512 : (h + 1) * 512],
                    start=True,
                    stop=True,
                )
                y = ypool.tile([P, 512], F32, name="y")
                if k % 2 == 0:
                    nc.vector.tensor_scalar_add(out=y[:], in0=yp[:], scalar1=b3f[:, ot : ot + 1])
                else:
                    nc.scalar.activation(out=y[:], in_=yp[:], func=IDENTITY, bias=b3f[:, ot : ot + 1], scale=1.0)
                nc.sync.dma_start(out=outv[:, ot, h * 512 : (h + 1) * 512], in_=y[:])
                k += 1
